import numpy as np
import ml_dtypes


def mxq(x, axis, fmt="e4m3"):
    dtype, down = {"e4m3": (ml_dtypes.float8_e4m3fn, 7), "e5m2": (ml_dtypes.float8_e5m2, 14)}[fmt]
    v = np.moveaxis(np.asarray(x, np.float32).astype(ml_dtypes.bfloat16).astype(np.float64), axis, -1)
    blocks = v.reshape(v.shape[:-1] + (-1, 32))
    amax = np.abs(blocks).max(-1, keepdims=True)
    byte = np.maximum(np.where(amax > 0, np.frexp(amax)[1] - 1 + 127, 0) - down, 1)
    scale = np.exp2(byte - 127.0)
    codes = (blocks / scale).astype(np.float32).astype(dtype).astype(np.float64)
    return np.moveaxis((codes * scale).reshape(v.shape), -1, axis)


WIDE = False


def mx_kscale(k):
    if not WIDE:
        return np.ones(k)
    levels = np.array([10, -10, 5, -5, 0])
    a = np.random.permutation(np.resize(levels, k // 512 * 4)).reshape(k // 512, 4)
    idx = np.arange(k)
    return np.exp2(a[idx // 512, idx % 128 // 32])


BF16 = ml_dtypes.bfloat16


def bf(x):
    return np.asarray(x, np.float32).astype(BF16)


def f64(x):
    return np.asarray(x).astype(np.float64)


B, N, D, HEAD, HALF = 1, 1024, 512, 1024, 512


def setup_inputs():
    t = mx_kscale(N)
    r = np.square(np.maximum(np.random.standard_normal((B, N, HALF)), 0.0))
    r = r / np.sqrt(np.sum(np.square(r), axis=-1, keepdims=True))
    return {"xr_n": bf(r / t[None, :, None]),
            "V": bf(np.random.standard_normal((N, N)) * 6.0 * np.sqrt(HALF / N) * t[:, None] * (t * t)[None, :])}


def reference(xr_n, V):
    xr = f64(xr_n)
    xq = mxq(xr, 2, "e4m3")
    cos = xq @ xq.transpose(0, 2, 1)
    weighted = f64(V)[None, :, :] * cos
    return mxq(weighted, 2, "e4m3") @ mxq(xr, 1, "e4m3")

@@ -1,0 +1,206 @@
+from contextlib import ExitStack
+
+import concourse.mybir as mybir
+from concourse.masks import make_identity
+
+BF16 = mybir.dt.bfloat16
+F32 = mybir.dt.float32
+U32 = mybir.dt.uint32
+U8 = mybir.dt.uint8
+FP8X4 = mybir.dt.float8_e4m3fn_x4
+
+P = 128
+PACK = 4
+K_PASS = P * PACK
+POSITIONS = 1024
+FEATURES = 512
+CHUNK = 2 * P
+CHUNKS = POSITIONS // CHUNK
+BLOCKS = POSITIONS // P
+PASSES = POSITIONS // K_PASS
+AHEAD = 2
+
+FLOPS = 2 * 2 * POSITIONS * POSITIONS * FEATURES
+
+
+def tile_avey_pb_kernel(tc, xr_n, V, out):
+    nc = tc.nc
+    x_rows = xr_n.flatten_outer_dims().rearrange("(a j e) f -> j a e f", a=CHUNKS, e=2)
+    v_rows = V.rearrange("(a j e) m -> j a e m", a=CHUNKS, e=2)
+    out_rows = out.flatten_outer_dims().rearrange("(a j e) f -> j a e f", a=CHUNKS, e=2)
+
+    with ExitStack() as ctx:
+        keep = ctx.enter_context(tc.tile_pool(name="keep", bufs=1))
+        work = ctx.enter_context(tc.tile_pool(name="work", bufs=4))
+        psum_turn = ctx.enter_context(tc.psum_pool(name="psum_turn", bufs=2))
+        psum_cos = ctx.enter_context(tc.psum_pool(name="psum_cos", bufs=AHEAD * PASSES))
+        psum_out = ctx.enter_context(tc.psum_pool(name="psum_out", bufs=2))
+
+        identity = keep.tile([P, P], F32)
+        make_identity(nc, identity[:])
+
+        x_raw = keep.tile([P, BLOCKS * FEATURES], BF16, align_bytes=64)
+        v_raw = keep.tile([P, BLOCKS * POSITIONS], BF16, align_bytes=64)
+        for a in range(CHUNKS):
+            nc.sync.dma_start(
+                out=x_raw[:, a * 2 * FEATURES : (a + 1) * 2 * FEATURES].rearrange(
+                    "p (e f) -> p e f", e=2
+                ),
+                in_=x_rows[:, a],
+            )
+        for a in range(CHUNKS):
+            nc.sync.dma_start(
+                out=v_raw[:, a * 2 * POSITIONS : (a + 1) * 2 * POSITIONS].rearrange(
+                    "p (e m) -> p e m", e=2
+                ),
+                in_=v_rows[:, a],
+            )
+        x_words = x_raw[:].bitcast(F32)
+        v_words = v_raw[:].bitcast(F32)
+
+        xf_grouped = keep.tile([P, POSITIONS * PACK], BF16, align_bytes=64)
+        xf_codes = keep.tile([P, POSITIONS], U32, align_bytes=64)
+        xf_scales = keep.tile([P, POSITIONS], U8, align_bytes=64)
+        xp_grouped = keep.tile([P, PASSES * FEATURES * PACK], BF16, align_bytes=64)
+        xp_codes = keep.tile([P, PASSES * FEATURES], U32, align_bytes=64)
+        xp_scales = keep.tile([P, PASSES * FEATURES], U8, align_bytes=64)
+        vt = keep.tile([P, BLOCKS * PASSES * P * PACK], BF16, align_bytes=64)
+        w_codes = keep.tile([P, BLOCKS * PASSES * P], U32, align_bytes=64)
+        w_scales = keep.tile([P, BLOCKS * PASSES * P], U8, align_bytes=64)
+
+        def turn_x(a):
+            turned = psum_turn.tile([P, 2, 2, P], F32, name="turned")
+            for h in range(2):
+                for e in range(2):
+                    first = (2 * a + e) * (FEATURES // 2) + h * P
+                    nc.tensor.transpose(
+                        turned[:, h, e, :], x_words[:, first : first + P], identity[:]
+                    )
+            nc.scalar.copy(
+                out=xf_grouped[:]
+                .bitcast(F32)[:, a * CHUNK * 2 : (a + 1) * CHUNK * 2]
+                .rearrange("p (i h) -> p i h", h=2),
+                in_=turned[:].rearrange("p h e j -> p (e j) h"),
+            )
+
+        def quantise_x_along_features(a):
+            cols = slice(a * CHUNK, (a + 1) * CHUNK)
+            nc.vector.quantize_mx(
+                out=xf_codes[:, cols].bitcast(FP8X4),
+                scales=xf_scales[:, cols],
+                in_=xf_grouped[:, a * CHUNK * PACK : (a + 1) * CHUNK * PACK],
+            )
+
+        def regroup_x_for_positions(c):
+            span = slice(c * FEATURES * PACK, (c + 1) * FEATURES * PACK)
+            nc.vector.tensor_copy(
+                out=xp_grouped[:, span].rearrange("p (q i t) -> p q t i", i=4, t=PACK),
+                in_=x_raw[:, span].rearrange("p (t q i) -> p q t i", i=4, t=PACK),
+            )
+
+        def quantise_x_along_positions(c):
+            cols = slice(c * FEATURES, (c + 1) * FEATURES)
+            nc.vector.quantize_mx(
+                out=xp_codes[:, cols].bitcast(FP8X4),
+                scales=xp_scales[:, cols],
+                in_=xp_grouped[:, c * FEATURES * PACK : (c + 1) * FEATURES * PACK],
+            )
+
+        def turn_v(b):
+            turned = psum_turn.tile([P, PASSES * 2, P], F32, name="turned")
+            for w in range(PASSES * 2):
+                first = b * (POSITIONS // 2) + w * P
+                nc.tensor.transpose(turned[:, w, :], v_words[:, first : first + P], identity[:])
+            nc.scalar.copy(
+                out=vt[:]
+                .bitcast(F32)[:, b * PASSES * P * 2 : (b + 1) * PASSES * P * 2]
+                .rearrange("p (c n u) -> p c n u", c=PASSES, u=2),
+                in_=turned[:].rearrange("p (c u) n -> p c n u", u=2),
+            )
+
+        cos_banks = {}
+
+        def cosines(b):
+            n_cols = slice(b * P, (b + 1) * P)
+            for c in range(PASSES):
+                bank = psum_cos.tile([P, PACK, P], F32, name="cos_bank")
+                for t in range(PACK):
+                    m_cols = slice((c * PACK + t) * P, (c * PACK + t + 1) * P)
+                    nc.tensor.matmul_mx(
+                        out=bank[:, t, :],
+                        lhsT=xf_codes[:, m_cols].bitcast(FP8X4),
+                        lhsT_scale=xf_scales[:, m_cols],
+                        rhs=xf_codes[:, n_cols].bitcast(FP8X4),
+                        rhs_scale=xf_scales[:, n_cols],
+                        start=True,
+                        stop=True,
+                    )
+                cos_banks[(b, c)] = bank
+
+        weighted_tiles = {}
+
+        def weigh(b, c):
+            weighted = work.tile([P, P, PACK], BF16, align_bytes=64, name="weighted")
+            first = (b * PASSES + c) * P * PACK
+            nc.vector.tensor_tensor(
+                out=weighted[:],
+                in0=cos_banks[(b, c)][:].rearrange("p t n -> p n t"),
+                in1=vt[:, first : first + P * PACK].rearrange("p (n t) -> p n t", t=PACK),
+                op=mybir.AluOpType.mult,
+            )
+            weighted_tiles[(b, c)] = weighted
+
+        def quantise_weighted(b, c):
+            cols = slice((b * PASSES + c) * P, (b * PASSES + c + 1) * P)
+            nc.vector.quantize_mx(
+                out=w_codes[:, cols].bitcast(FP8X4),
+                scales=w_scales[:, cols],
+                in_=weighted_tiles[(b, c)][:].rearrange("p n t -> p (n t)"),
+            )
+
+        def project(b):
+            acc = psum_out.tile([P, FEATURES], F32, name="acc")
+            for c in range(PASSES):
+                n_cols = slice((b * PASSES + c) * P, (b * PASSES + c + 1) * P)
+                f_cols = slice(c * FEATURES, (c + 1) * FEATURES)
+                nc.tensor.matmul_mx(
+                    out=acc[:],
+                    lhsT=w_codes[:, n_cols].bitcast(FP8X4),
+                    lhsT_scale=w_scales[:, n_cols],
+                    rhs=xp_codes[:, f_cols].bitcast(FP8X4),
+                    rhs_scale=xp_scales[:, f_cols],
+                    start=(c == 0),
+                    stop=(c == PASSES - 1),
+                )
+            result = work.tile([P, FEATURES], F32, name="result")
+            nc.scalar.copy(out=result[:], in_=acc[:])
+            nc.sync.dma_start(out=out_rows[:, b // 2, b % 2, :], in_=result[:])
+
+        for c in range(PASSES):
+            for a in (2 * c, 2 * c + 1):
+                turn_x(a)
+            for a in (2 * c, 2 * c + 1):
+                quantise_x_along_features(a)
+            regroup_x_for_positions(c)
+        for c in range(PASSES):
+            quantise_x_along_positions(c)
+
+        for b in range(AHEAD):
+            turn_v(b)
+        for b in range(AHEAD):
+            cosines(b)
+        for b in range(AHEAD, BLOCKS):
+            turn_v(b)
+
+        for b in range(BLOCKS):
+            weigh(b, 0)
+            if b > 0:
+                quantise_weighted(b - 1, 1)
+            weigh(b, 1)
+            quantise_weighted(b, 0)
+            if b > 0:
+                project(b - 1)
+            if b + AHEAD < BLOCKS:
+                cosines(b + AHEAD)
+        quantise_weighted(BLOCKS - 1, 1)
+        project(BLOCKS - 1)

@@ -19,6 +19,7 @@ CHUNKS = POSITIONS // CHUNK
 BLOCKS = POSITIONS // P
 PASSES = POSITIONS // K_PASS
 AHEAD = 2
+TURNED_AHEAD = 4
 
 FLOPS = 2 * 2 * POSITIONS * POSITIONS * FEATURES
 
@@ -35,6 +36,7 @@ def tile_avey_pb_kernel(tc, xr_n, V, out):
         psum_turn = ctx.enter_context(tc.psum_pool(name="psum_turn", bufs=2))
         psum_cos = ctx.enter_context(tc.psum_pool(name="psum_cos", bufs=AHEAD * PASSES))
         psum_out = ctx.enter_context(tc.psum_pool(name="psum_out", bufs=2))
+        ctx.enter_context(tc.manual_schedule())
 
         identity = keep.tile([P, P], F32)
         make_identity(nc, identity[:])
@@ -179,9 +181,9 @@ def tile_avey_pb_kernel(tc, xr_n, V, out):
         for c in range(PASSES):
             for a in (2 * c, 2 * c + 1):
                 turn_x(a)
+            regroup_x_for_positions(c)
             for a in (2 * c, 2 * c + 1):
                 quantise_x_along_features(a)
-            regroup_x_for_positions(c)
         for c in range(PASSES):
             quantise_x_along_positions(c)
 
@@ -189,7 +191,7 @@ def tile_avey_pb_kernel(tc, xr_n, V, out):
             turn_v(b)
         for b in range(AHEAD):
             cosines(b)
-        for b in range(AHEAD, BLOCKS):
+        for b in range(AHEAD, TURNED_AHEAD):
             turn_v(b)
 
         for b in range(BLOCKS):
@@ -202,5 +204,8 @@ def tile_avey_pb_kernel(tc, xr_n, V, out):
                 project(b - 1)
             if b + AHEAD < BLOCKS:
                 cosines(b + AHEAD)
+            if b % 2 == 0 and b + TURNED_AHEAD < BLOCKS:
+                turn_v(b + TURNED_AHEAD)
+                turn_v(b + TURNED_AHEAD + 1)
         quantise_weighted(BLOCKS - 1, 1)
         project(BLOCKS - 1)

@@ -71,7 +71,10 @@ def tile_avey_pb_kernel(tc, xr_n, V, out):
         w_scales = keep.tile([P, BLOCKS * PASSES * P], U8, align_bytes=64)
 
         def turn_x(a):
-            turned = psum_turn.tile([P, 2, 2, P], F32, name="turned")
+            if a % 2 == 0:
+                turned = psum_turn.tile([P, 2, 2, P], F32, name="turned")
+            else:
+                turned = psum_out.tile([P, 2, 2, P], F32, name="acc")
             for h in range(2):
                 for e in range(2):
                     first = (2 * a + e) * (FEATURES // 2) + h * P
@@ -93,11 +96,12 @@ def tile_avey_pb_kernel(tc, xr_n, V, out):
                 in_=xf_grouped[:, a * CHUNK * PACK : (a + 1) * CHUNK * PACK],
             )
 
-        def regroup_x_for_positions(c):
+        def regroup_x_for_positions(copy, c, quarters):
             span = slice(c * FEATURES * PACK, (c + 1) * FEATURES * PACK)
-            nc.vector.tensor_copy(
-                out=xp_grouped[:, span].rearrange("p (q i t) -> p q t i", i=4, t=PACK),
-                in_=x_raw[:, span].rearrange("p (t q i) -> p q t i", i=4, t=PACK),
+            cols = slice(quarters[0] * FEATURES // 16, (quarters[-1] + 1) * FEATURES // 16)
+            copy(
+                out=xp_grouped[:, span].rearrange("p (q i t) -> p q t i", i=4, t=PACK)[:, cols],
+                in_=x_raw[:, span].rearrange("p (t q i) -> p q t i", i=4, t=PACK)[:, cols],
             )
 
         def quantise_x_along_positions(c):
@@ -178,21 +182,22 @@ def tile_avey_pb_kernel(tc, xr_n, V, out):
             nc.scalar.copy(out=result[:], in_=acc[:])
             nc.sync.dma_start(out=out_rows[:, b // 2, b % 2, :], in_=result[:])
 
-        for c in range(PASSES):
-            for a in (2 * c, 2 * c + 1):
-                turn_x(a)
-            regroup_x_for_positions(c)
-            for a in (2 * c, 2 * c + 1):
-                quantise_x_along_features(a)
-        for c in range(PASSES):
-            quantise_x_along_positions(c)
+        for a in range(CHUNKS):
+            turn_x(a)
+        regroup_x_for_positions(nc.vector.tensor_copy, 0, range(4))
+        for a in (0, 1):
+            quantise_x_along_features(a)
+        quantise_x_along_positions(0)
+        for a in (2, 3):
+            quantise_x_along_features(a)
 
         for b in range(AHEAD):
             turn_v(b)
+            regroup_x_for_positions(nc.scalar.copy, 1, range(2 * b, 2 * b + 1))
+            regroup_x_for_positions(nc.scalar.copy, 1, range(2 * b + 1, 2 * b + 2))
         for b in range(AHEAD):
             cosines(b)
-        for b in range(AHEAD, TURNED_AHEAD):
-            turn_v(b)
+        turn_v(AHEAD)
 
         for b in range(BLOCKS):
             weigh(b, 0)
@@ -200,12 +205,16 @@ def tile_avey_pb_kernel(tc, xr_n, V, out):
                 quantise_weighted(b - 1, 1)
             weigh(b, 1)
             quantise_weighted(b, 0)
-            if b > 0:
-                project(b - 1)
+            if b == 1:
+                quantise_x_along_positions(1)
             if b + AHEAD < BLOCKS:
                 cosines(b + AHEAD)
-            if b % 2 == 0 and b + TURNED_AHEAD < BLOCKS:
+            if b == 0:
+                turn_v(AHEAD + 1)
+            if b % 2 == 1 and b + TURNED_AHEAD <= BLOCKS:
+                turn_v(b + TURNED_AHEAD - 1)
                 turn_v(b + TURNED_AHEAD)
-                turn_v(b + TURNED_AHEAD + 1)
+            if b > 0:
+                project(b - 1)
         quantise_weighted(BLOCKS - 1, 1)
         project(BLOCKS - 1)

@@ -185,16 +185,18 @@ def tile_avey_pb_kernel(tc, xr_n, V, out):
         for a in range(CHUNKS):
             turn_x(a)
         regroup_x_for_positions(nc.vector.tensor_copy, 0, range(4))
-        for a in (0, 1):
-            quantise_x_along_features(a)
+        quantise_x_along_features(0)
+        regroup_x_for_positions(nc.vector.tensor_copy, 1, range(0, 1))
+        quantise_x_along_features(1)
         quantise_x_along_positions(0)
-        for a in (2, 3):
-            quantise_x_along_features(a)
+        quantise_x_along_features(2)
+        quantise_x_along_features(3)
+        regroup_x_for_positions(nc.vector.tensor_copy, 1, range(1, 2))
 
         for b in range(AHEAD):
             turn_v(b)
-            regroup_x_for_positions(nc.scalar.copy, 1, range(2 * b, 2 * b + 1))
-            regroup_x_for_positions(nc.scalar.copy, 1, range(2 * b + 1, 2 * b + 2))
+        for quarter in (2, 3):
+            regroup_x_for_positions(nc.scalar.copy, 1, range(quarter, quarter + 1))
         for b in range(AHEAD):
             cosines(b)
         turn_v(AHEAD)

@@ -182,6 +182,29 @@ def tile_avey_pb_kernel(tc, xr_n, V, out):
             nc.scalar.copy(out=result[:], in_=acc[:])
             nc.sync.dma_start(out=out_rows[:, b // 2, b % 2, :], in_=result[:])
 
+        def project_in_halves(b):
+            half = FEATURES // 2
+            accs = [psum_turn.tile([P, half], F32, name="turned") for side in range(2)]
+            for c in range(PASSES):
+                n_cols = slice((b * PASSES + c) * P, (b * PASSES + c + 1) * P)
+                for side in range(2):
+                    f_cols = slice(c * FEATURES + side * half, c * FEATURES + (side + 1) * half)
+                    nc.tensor.matmul_mx(
+                        out=accs[side][:],
+                        lhsT=w_codes[:, n_cols].bitcast(FP8X4),
+                        lhsT_scale=w_scales[:, n_cols],
+                        rhs=xp_codes[:, f_cols].bitcast(FP8X4),
+                        rhs_scale=xp_scales[:, f_cols],
+                        start=(c == 0),
+                        stop=(c == PASSES - 1),
+                    )
+            for side, copy in ((0, nc.scalar.copy), (1, nc.vector.tensor_copy)):
+                result = work.tile([P, half], F32, name="result_half")
+                copy(out=result[:], in_=accs[side][:])
+                nc.sync.dma_start(
+                    out=out_rows[:, b // 2, b % 2, side * half : (side + 1) * half], in_=result[:]
+                )
+
         for a in range(CHUNKS):
             turn_x(a)
         regroup_x_for_positions(nc.vector.tensor_copy, 0, range(4))
@@ -219,4 +242,4 @@ def tile_avey_pb_kernel(tc, xr_n, V, out):
             if b > 0:
                 project(b - 1)
         quantise_weighted(BLOCKS - 1, 1)
-        project(BLOCKS - 1)
+        project_in_halves(BLOCKS - 1)

@@ -19,6 +19,7 @@ CHUNKS = POSITIONS // CHUNK
 BLOCKS = POSITIONS // P
 PASSES = POSITIONS // K_PASS
 AHEAD = 2
+ON_GPSIMD = ((3, 1), (5, 1))
 TURNED_AHEAD = 4
 
 FLOPS = 2 * 2 * POSITIONS * POSITIONS * FEATURES
@@ -33,6 +34,7 @@ def tile_avey_pb_kernel(tc, xr_n, V, out):
     with ExitStack() as ctx:
         keep = ctx.enter_context(tc.tile_pool(name="keep", bufs=1))
         work = ctx.enter_context(tc.tile_pool(name="work", bufs=4))
+        handed = ctx.enter_context(tc.tile_pool(name="handed", bufs=1))
         psum_turn = ctx.enter_context(tc.psum_pool(name="psum_turn", bufs=2))
         psum_cos = ctx.enter_context(tc.psum_pool(name="psum_cos", bufs=AHEAD * PASSES))
         psum_out = ctx.enter_context(tc.psum_pool(name="psum_out", bufs=2))
@@ -126,9 +128,9 @@ def tile_avey_pb_kernel(tc, xr_n, V, out):
 
         cos_banks = {}
 
-        def cosines(b):
+        def cosines(b, passes=range(PASSES)):
             n_cols = slice(b * P, (b + 1) * P)
-            for c in range(PASSES):
+            for c in passes:
                 bank = psum_cos.tile([P, PACK, P], F32, name="cos_bank")
                 for t in range(PACK):
                     m_cols = slice((c * PACK + t) * P, (c * PACK + t + 1) * P)
@@ -146,11 +148,24 @@ def tile_avey_pb_kernel(tc, xr_n, V, out):
         weighted_tiles = {}
 
         def weigh(b, c):
-            weighted = work.tile([P, P, PACK], BF16, align_bytes=64, name="weighted")
+            if b % 2 == 0:
+                weighted = work.tile([P, P, PACK], BF16, align_bytes=64, name="weighted")
+            else:
+                turn = b // 2 if c == 0 else b // 2 + 2
+                weighted = handed.tile(
+                    [P, P, PACK], BF16, align_bytes=64, name="handed_on_%d" % (turn % 3)
+                )
             first = (b * PASSES + c) * P * PACK
-            nc.vector.tensor_tensor(
+            cos = cos_banks[(b, c)][:].rearrange("p t n -> p n t")
+            multiply = nc.vector.tensor_tensor
+            if (b, c) in ON_GPSIMD:
+                copied = work.tile([P, P, PACK], F32, name="copied")
+                nc.scalar.copy(out=copied[:], in_=cos)
+                cos = copied[:]
+                multiply = nc.gpsimd.tensor_tensor
+            multiply(
                 out=weighted[:],
-                in0=cos_banks[(b, c)][:].rearrange("p t n -> p n t"),
+                in0=cos,
                 in1=vt[:, first : first + P * PACK].rearrange("p (n t) -> p n t", t=PACK),
                 op=mybir.AluOpType.mult,
             )
@@ -165,7 +180,10 @@ def tile_avey_pb_kernel(tc, xr_n, V, out):
             )
 
         def project(b):
-            acc = psum_out.tile([P, FEATURES], F32, name="acc")
+            if b == BLOCKS - 3:
+                acc = psum_turn.tile([P, FEATURES], F32, name="turned")
+            else:
+                acc = psum_out.tile([P, FEATURES], F32, name="acc")
             for c in range(PASSES):
                 n_cols = slice((b * PASSES + c) * P, (b * PASSES + c + 1) * P)
                 f_cols = slice(c * FEATURES, (c + 1) * FEATURES)
@@ -184,7 +202,7 @@ def tile_avey_pb_kernel(tc, xr_n, V, out):
 
         def project_in_halves(b):
             half = FEATURES // 2
-            accs = [psum_turn.tile([P, half], F32, name="turned") for side in range(2)]
+            accs = [psum_cos.tile([P, half], F32, name="cos_bank") for side in range(2)]
             for c in range(PASSES):
                 n_cols = slice((b * PASSES + c) * P, (b * PASSES + c + 1) * P)
                 for side in range(2):
@@ -224,22 +242,51 @@ def tile_avey_pb_kernel(tc, xr_n, V, out):
             cosines(b)
         turn_v(AHEAD)
 
-        for b in range(BLOCKS):
+        weigh(0, 0)
+        weigh(0, 1)
+        quantise_weighted(0, 0)
+        cosines(2)
+        turn_v(3)
+        weigh(1, 0)
+        quantise_weighted(0, 1)
+        weigh(1, 1)
+        quantise_weighted(1, 0)
+        quantise_x_along_positions(1)
+        cosines(3, passes=(1, 0))
+        weigh(3, 1)
+        turn_v(4)
+        turn_v(5)
+        project(0)
+
+        for b in (2, 4):
             weigh(b, 0)
-            if b > 0:
-                quantise_weighted(b - 1, 1)
             weigh(b, 1)
+            weigh(b + 1, 0)
+            quantise_weighted(b - 1, 1)
             quantise_weighted(b, 0)
-            if b == 1:
-                quantise_x_along_positions(1)
-            if b + AHEAD < BLOCKS:
-                cosines(b + AHEAD)
-            if b == 0:
-                turn_v(AHEAD + 1)
-            if b % 2 == 1 and b + TURNED_AHEAD <= BLOCKS:
-                turn_v(b + TURNED_AHEAD - 1)
-                turn_v(b + TURNED_AHEAD)
-            if b > 0:
-                project(b - 1)
-        quantise_weighted(BLOCKS - 1, 1)
-        project_in_halves(BLOCKS - 1)
+            quantise_weighted(b, 1)
+            quantise_weighted(b + 1, 0)
+            cosines(b + 2)
+            if b == 2:
+                cosines(b + 3, passes=(1, 0))
+                weigh(b + 3, 1)
+            else:
+                cosines(b + 3)
+            if b == 2:
+                turn_v(6)
+                turn_v(7)
+            project(b - 1)
+            project(b)
+
+        weigh(6, 0)
+        quantise_weighted(5, 1)
+        weigh(6, 1)
+        quantise_weighted(6, 0)
+        project(5)
+        weigh(7, 0)
+        quantise_weighted(6, 1)
+        weigh(7, 1)
+        quantise_weighted(7, 0)
+        project(6)
+        quantise_weighted(7, 1)
+        project_in_halves(7)

@@ -20,6 +20,7 @@ BLOCKS = POSITIONS // P
 PASSES = POSITIONS // K_PASS
 AHEAD = 2
 ON_GPSIMD = ((3, 1), (5, 1))
+WARM_UP = 12
 TURNED_AHEAD = 4
 
 FLOPS = 2 * 2 * POSITIONS * POSITIONS * FEATURES
@@ -179,7 +180,7 @@ def tile_avey_pb_kernel(tc, xr_n, V, out):
                 in_=weighted_tiles[(b, c)][:].rearrange("p n t -> p (n t)"),
             )
 
-        def project(b):
+        def project(b, copy=nc.scalar.copy):
             if b == BLOCKS - 3:
                 acc = psum_turn.tile([P, FEATURES], F32, name="turned")
             else:
@@ -196,8 +197,8 @@ def tile_avey_pb_kernel(tc, xr_n, V, out):
                     start=(c == 0),
                     stop=(c == PASSES - 1),
                 )
-            result = work.tile([P, FEATURES], F32, name="result")
-            nc.scalar.copy(out=result[:], in_=acc[:])
+            result = work.tile([P, FEATURES], F32, name="result", bufs=BLOCKS)
+            copy(out=result[:], in_=acc[:])
             nc.sync.dma_start(out=out_rows[:, b // 2, b % 2, :], in_=result[:])
 
         def project_in_halves(b):
@@ -222,6 +223,14 @@ def tile_avey_pb_kernel(tc, xr_n, V, out):
                 nc.sync.dma_start(
                     out=out_rows[:, b // 2, b % 2, side * half : (side + 1) * half], in_=result[:]
                 )
+
+        idle = keep.tile([P, P], BF16)
+        nc.vector.memset(idle[:], 0.0)
+        unread = psum_cos.tile([P, PACK, P], F32, name="cos_bank")
+        for i in range(WARM_UP):
+            nc.tensor.matmul(
+                unread[:, i % PACK, :], lhsT=idle[:], rhs=idle[:], start=True, stop=True
+            )
 
         for a in range(CHUNKS):
             turn_x(a)
@@ -270,13 +279,14 @@ def tile_avey_pb_kernel(tc, xr_n, V, out):
             if b == 2:
                 cosines(b + 3, passes=(1, 0))
                 weigh(b + 3, 1)
-            else:
-                cosines(b + 3)
-            if b == 2:
                 turn_v(6)
                 turn_v(7)
+            else:
+                project(b - 2)
+                cosines(b + 3)
             project(b - 1)
-            project(b)
+            if b == 4:
+                project(b)
 
         weigh(6, 0)
         quantise_weighted(5, 1)
@@ -287,6 +297,6 @@ def tile_avey_pb_kernel(tc, xr_n, V, out):
         quantise_weighted(6, 1)
         weigh(7, 1)
         quantise_weighted(7, 0)
-        project(6)
         quantise_weighted(7, 1)
+        project(6, copy=nc.vector.tensor_copy)
         project_in_halves(7)

@@ -19,7 +19,6 @@ CHUNKS = POSITIONS // CHUNK
 BLOCKS = POSITIONS // P
 PASSES = POSITIONS // K_PASS
 AHEAD = 2
-ON_GPSIMD = ((3, 1), (5, 1))
 WARM_UP = 12
 TURNED_AHEAD = 4
 
@@ -37,7 +36,7 @@ def tile_avey_pb_kernel(tc, xr_n, V, out):
         work = ctx.enter_context(tc.tile_pool(name="work", bufs=4))
         handed = ctx.enter_context(tc.tile_pool(name="handed", bufs=1))
         psum_turn = ctx.enter_context(tc.psum_pool(name="psum_turn", bufs=2))
-        psum_cos = ctx.enter_context(tc.psum_pool(name="psum_cos", bufs=AHEAD * PASSES))
+        psum_cos = ctx.enter_context(tc.psum_pool(name="psum_cos", bufs=1))
         psum_out = ctx.enter_context(tc.psum_pool(name="psum_out", bufs=2))
         ctx.enter_context(tc.manual_schedule())
 
@@ -132,7 +131,7 @@ def tile_avey_pb_kernel(tc, xr_n, V, out):
         def cosines(b, passes=range(PASSES)):
             n_cols = slice(b * P, (b + 1) * P)
             for c in passes:
-                bank = psum_cos.tile([P, PACK, P], F32, name="cos_bank")
+                bank = psum_cos.tile([P, PACK, P], F32, name="cos_%d" % (b % AHEAD * PASSES + (c if b < 3 or b % 2 == 0 else 1 - c)))
                 for t in range(PACK):
                     m_cols = slice((c * PACK + t) * P, (c * PACK + t + 1) * P)
                     nc.tensor.matmul_mx(
@@ -145,6 +144,13 @@ def tile_avey_pb_kernel(tc, xr_n, V, out):
                         stop=True,
                     )
                 cos_banks[(b, c)] = bank
+
+        copied_cos = {}
+
+        def bring_to_sbuf(b, c):
+            copied = work.tile([P, P, PACK], F32, name="copied")
+            nc.scalar.copy(out=copied[:], in_=cos_banks[(b, c)][:].rearrange("p t n -> p n t"))
+            copied_cos[(b, c)] = copied
 
         weighted_tiles = {}
 
@@ -159,10 +165,8 @@ def tile_avey_pb_kernel(tc, xr_n, V, out):
             first = (b * PASSES + c) * P * PACK
             cos = cos_banks[(b, c)][:].rearrange("p t n -> p n t")
             multiply = nc.vector.tensor_tensor
-            if (b, c) in ON_GPSIMD:
-                copied = work.tile([P, P, PACK], F32, name="copied")
-                nc.scalar.copy(out=copied[:], in_=cos)
-                cos = copied[:]
+            if (b, c) in copied_cos:
+                cos = copied_cos[(b, c)][:]
                 multiply = nc.gpsimd.tensor_tensor
             multiply(
                 out=weighted[:],
@@ -203,7 +207,7 @@ def tile_avey_pb_kernel(tc, xr_n, V, out):
 
         def project_in_halves(b):
             half = FEATURES // 2
-            accs = [psum_cos.tile([P, half], F32, name="cos_bank") for side in range(2)]
+            accs = [psum_cos.tile([P, half], F32, name="cos_%d" % side) for side in range(2)]
             for c in range(PASSES):
                 n_cols = slice((b * PASSES + c) * P, (b * PASSES + c + 1) * P)
                 for side in range(2):
@@ -226,7 +230,7 @@ def tile_avey_pb_kernel(tc, xr_n, V, out):
 
         idle = keep.tile([P, P], BF16)
         nc.vector.memset(idle[:], 0.0)
-        unread = psum_cos.tile([P, PACK, P], F32, name="cos_bank")
+        unread = psum_cos.tile([P, PACK, P], F32, name="cos_0")
         for i in range(WARM_UP):
             nc.tensor.matmul(
                 unread[:, i % PACK, :], lhsT=idle[:], rhs=idle[:], start=True, stop=True
@@ -262,9 +266,12 @@ def tile_avey_pb_kernel(tc, xr_n, V, out):
         quantise_weighted(1, 0)
         quantise_x_along_positions(1)
         cosines(3, passes=(1, 0))
+        bring_to_sbuf(3, 1)
         weigh(3, 1)
         turn_v(4)
         turn_v(5)
+        cosines(5, passes=(1,))
+        bring_to_sbuf(5, 1)
         project(0)
 
         for b in (2, 4):
@@ -277,8 +284,8 @@ def tile_avey_pb_kernel(tc, xr_n, V, out):
             quantise_weighted(b + 1, 0)
             cosines(b + 2)
             if b == 2:
-                cosines(b + 3, passes=(1, 0))
                 weigh(b + 3, 1)
+                cosines(b + 3, passes=(0,))
                 turn_v(6)
                 turn_v(7)
             else:

from contextlib import ExitStack

import concourse.mybir as mybir
from concourse.masks import make_identity

BF16 = mybir.dt.bfloat16
F32 = mybir.dt.float32
U32 = mybir.dt.uint32
U8 = mybir.dt.uint8
FP8X4 = mybir.dt.float8_e4m3fn_x4

P = 128
PACK = 4
K_PASS = P * PACK
POSITIONS = 1024
FEATURES = 512
CHUNK = 2 * P
CHUNKS = POSITIONS // CHUNK
BLOCKS = POSITIONS // P
PASSES = POSITIONS // K_PASS
AHEAD = 2
WARM_UP = 12
TURNED_AHEAD = 4

FLOPS = 2 * 2 * POSITIONS * POSITIONS * FEATURES


def tile_avey_pb_kernel(tc, xr_n, V, out):
    nc = tc.nc
    x_rows = xr_n.flatten_outer_dims().rearrange("(a j e) f -> j a e f", a=CHUNKS, e=2)
    v_rows = V.rearrange("(a j e) m -> j a e m", a=CHUNKS, e=2)
    out_rows = out.flatten_outer_dims().rearrange("(a j e) f -> j a e f", a=CHUNKS, e=2)

    with ExitStack() as ctx:
        keep = ctx.enter_context(tc.tile_pool(name="keep", bufs=1))
        work = ctx.enter_context(tc.tile_pool(name="work", bufs=4))
        handed = ctx.enter_context(tc.tile_pool(name="handed", bufs=1))
        psum_turn = ctx.enter_context(tc.psum_pool(name="psum_turn", bufs=2))
        psum_cos = ctx.enter_context(tc.psum_pool(name="psum_cos", bufs=1))
        psum_out = ctx.enter_context(tc.psum_pool(name="psum_out", bufs=2))
        ctx.enter_context(tc.manual_schedule())

        identity = keep.tile([P, P], F32)
        make_identity(nc, identity[:])

        x_raw = keep.tile([P, BLOCKS * FEATURES], BF16, align_bytes=64)
        v_raw = keep.tile([P, BLOCKS * POSITIONS], BF16, align_bytes=64)
        for a in range(CHUNKS):
            nc.sync.dma_start(
                out=x_raw[:, a * 2 * FEATURES : (a + 1) * 2 * FEATURES].rearrange(
                    "p (e f) -> p e f", e=2
                ),
                in_=x_rows[:, a],
            )
        for a in range(CHUNKS):
            nc.sync.dma_start(
                out=v_raw[:, a * 2 * POSITIONS : (a + 1) * 2 * POSITIONS].rearrange(
                    "p (e m) -> p e m", e=2
                ),
                in_=v_rows[:, a],
            )
        x_words = x_raw[:].bitcast(F32)
        v_words = v_raw[:].bitcast(F32)

        xf_grouped = keep.tile([P, POSITIONS * PACK], BF16, align_bytes=64)
        xf_codes = keep.tile([P, POSITIONS], U32, align_bytes=64)
        xf_scales = keep.tile([P, POSITIONS], U8, align_bytes=64)
        xp_grouped = keep.tile([P, PASSES * FEATURES * PACK], BF16, align_bytes=64)
        xp_codes = keep.tile([P, PASSES * FEATURES], U32, align_bytes=64)
        xp_scales = keep.tile([P, PASSES * FEATURES], U8, align_bytes=64)
        vt = keep.tile([P, BLOCKS * PASSES * P * PACK], BF16, align_bytes=64)
        w_codes = keep.tile([P, BLOCKS * PASSES * P], U32, align_bytes=64)
        w_scales = keep.tile([P, BLOCKS * PASSES * P], U8, align_bytes=64)

        def turn_x(a):
            if a % 2 == 0:
                turned = psum_turn.tile([P, 2, 2, P], F32, name="turned")
            else:
                turned = psum_out.tile([P, 2, 2, P], F32, name="acc")
            for h in range(2):
                for e in range(2):
                    first = (2 * a + e) * (FEATURES // 2) + h * P
                    nc.tensor.transpose(
                        turned[:, h, e, :], x_words[:, first : first + P], identity[:]
                    )
            nc.scalar.copy(
                out=xf_grouped[:]
                .bitcast(F32)[:, a * CHUNK * 2 : (a + 1) * CHUNK * 2]
                .rearrange("p (i h) -> p i h", h=2),
                in_=turned[:].rearrange("p h e j -> p (e j) h"),
            )

        def quantise_x_along_features(a):
            cols = slice(a * CHUNK, (a + 1) * CHUNK)
            nc.vector.quantize_mx(
                out=xf_codes[:, cols].bitcast(FP8X4),
                scales=xf_scales[:, cols],
                in_=xf_grouped[:, a * CHUNK * PACK : (a + 1) * CHUNK * PACK],
            )

        def regroup_x_for_positions(copy, c, quarters):
            span = slice(c * FEATURES * PACK, (c + 1) * FEATURES * PACK)
            cols = slice(quarters[0] * FEATURES // 16, (quarters[-1] + 1) * FEATURES // 16)
            copy(
                out=xp_grouped[:, span].rearrange("p (q i t) -> p q t i", i=4, t=PACK)[:, cols],
                in_=x_raw[:, span].rearrange("p (t q i) -> p q t i", i=4, t=PACK)[:, cols],
            )

        def quantise_x_along_positions(c):
            cols = slice(c * FEATURES, (c + 1) * FEATURES)
            nc.vector.quantize_mx(
                out=xp_codes[:, cols].bitcast(FP8X4),
                scales=xp_scales[:, cols],
                in_=xp_grouped[:, c * FEATURES * PACK : (c + 1) * FEATURES * PACK],
            )

        def turn_v(b):
            turned = psum_turn.tile([P, PASSES * 2, P], F32, name="turned")
            for w in range(PASSES * 2):
                first = b * (POSITIONS // 2) + w * P
                nc.tensor.transpose(turned[:, w, :], v_words[:, first : first + P], identity[:])
            nc.scalar.copy(
                out=vt[:]
                .bitcast(F32)[:, b * PASSES * P * 2 : (b + 1) * PASSES * P * 2]
                .rearrange("p (c n u) -> p c n u", c=PASSES, u=2),
                in_=turned[:].rearrange("p (c u) n -> p c n u", u=2),
            )

        cos_banks = {}

        def cosines(b, passes=range(PASSES)):
            n_cols = slice(b * P, (b + 1) * P)
            for c in passes:
                bank = psum_cos.tile([P, PACK, P], F32, name="cos_%d" % (b % AHEAD * PASSES + (c if b < 3 or b % 2 == 0 else 1 - c)))
                for t in range(PACK):
                    m_cols = slice((c * PACK + t) * P, (c * PACK + t + 1) * P)
                    nc.tensor.matmul_mx(
                        out=bank[:, t, :],
                        lhsT=xf_codes[:, m_cols].bitcast(FP8X4),
                        lhsT_scale=xf_scales[:, m_cols],
                        rhs=xf_codes[:, n_cols].bitcast(FP8X4),
                        rhs_scale=xf_scales[:, n_cols],
                        start=True,
                        stop=True,
                    )
                cos_banks[(b, c)] = bank

        copied_cos = {}

        def bring_to_sbuf(b, c):
            copied = work.tile([P, P, PACK], F32, name="copied")
            nc.scalar.copy(out=copied[:], in_=cos_banks[(b, c)][:].rearrange("p t n -> p n t"))
            copied_cos[(b, c)] = copied

        weighted_tiles = {}

        def weigh(b, c):
            if b % 2 == 0:
                weighted = work.tile([P, P, PACK], BF16, align_bytes=64, name="weighted")
            else:
                turn = b // 2 if c == 0 else b // 2 + 2
                weighted = handed.tile(
                    [P, P, PACK], BF16, align_bytes=64, name="handed_on_%d" % (turn % 3)
                )
            first = (b * PASSES + c) * P * PACK
            cos = cos_banks[(b, c)][:].rearrange("p t n -> p n t")
            multiply = nc.vector.tensor_tensor
            if (b, c) in copied_cos:
                cos = copied_cos[(b, c)][:]
                multiply = nc.gpsimd.tensor_tensor
            multiply(
                out=weighted[:],
                in0=cos,
                in1=vt[:, first : first + P * PACK].rearrange("p (n t) -> p n t", t=PACK),
                op=mybir.AluOpType.mult,
            )
            weighted_tiles[(b, c)] = weighted

        def quantise_weighted(b, c):
            cols = slice((b * PASSES + c) * P, (b * PASSES + c + 1) * P)
            nc.vector.quantize_mx(
                out=w_codes[:, cols].bitcast(FP8X4),
                scales=w_scales[:, cols],
                in_=weighted_tiles[(b, c)][:].rearrange("p n t -> p (n t)"),
            )

        def project(b, copy=nc.scalar.copy):
            if b == BLOCKS - 3:
                acc = psum_turn.tile([P, FEATURES], F32, name="turned")
            else:
                acc = psum_out.tile([P, FEATURES], F32, name="acc")
            for c in range(PASSES):
                n_cols = slice((b * PASSES + c) * P, (b * PASSES + c + 1) * P)
                f_cols = slice(c * FEATURES, (c + 1) * FEATURES)
                nc.tensor.matmul_mx(
                    out=acc[:],
                    lhsT=w_codes[:, n_cols].bitcast(FP8X4),
                    lhsT_scale=w_scales[:, n_cols],
                    rhs=xp_codes[:, f_cols].bitcast(FP8X4),
                    rhs_scale=xp_scales[:, f_cols],
                    start=(c == 0),
                    stop=(c == PASSES - 1),
                )
            result = work.tile([P, FEATURES], F32, name="result", bufs=BLOCKS)
            copy(out=result[:], in_=acc[:])
            nc.sync.dma_start(out=out_rows[:, b // 2, b % 2, :], in_=result[:])

        def project_in_halves(b):
            half = FEATURES // 2
            accs = [psum_cos.tile([P, half], F32, name="cos_%d" % side) for side in range(2)]
            for c in range(PASSES):
                n_cols = slice((b * PASSES + c) * P, (b * PASSES + c + 1) * P)
                for side in range(2):
                    f_cols = slice(c * FEATURES + side * half, c * FEATURES + (side + 1) * half)
                    nc.tensor.matmul_mx(
                        out=accs[side][:],
                        lhsT=w_codes[:, n_cols].bitcast(FP8X4),
                        lhsT_scale=w_scales[:, n_cols],
                        rhs=xp_codes[:, f_cols].bitcast(FP8X4),
                        rhs_scale=xp_scales[:, f_cols],
                        start=(c == 0),
                        stop=(c == PASSES - 1),
                    )
            for side, copy in ((0, nc.scalar.copy), (1, nc.vector.tensor_copy)):
                result = work.tile([P, half], F32, name="result_half")
                copy(out=result[:], in_=accs[side][:])
                nc.sync.dma_start(
                    out=out_rows[:, b // 2, b % 2, side * half : (side + 1) * half], in_=result[:]
                )

        idle = keep.tile([P, P], BF16)
        nc.vector.memset(idle[:], 0.0)
        unread = psum_cos.tile([P, PACK, P], F32, name="cos_0")
        for i in range(WARM_UP):
            nc.tensor.matmul(
                unread[:, i % PACK, :], lhsT=idle[:], rhs=idle[:], start=True, stop=True
            )

        for a in range(CHUNKS):
            turn_x(a)
        regroup_x_for_positions(nc.vector.tensor_copy, 0, range(4))
        quantise_x_along_features(0)
        regroup_x_for_positions(nc.vector.tensor_copy, 1, range(0, 1))
        quantise_x_along_features(1)
        quantise_x_along_positions(0)
        quantise_x_along_features(2)
        quantise_x_along_features(3)
        regroup_x_for_positions(nc.vector.tensor_copy, 1, range(1, 2))

        for b in range(AHEAD):
            turn_v(b)
        for quarter in (2, 3):
            regroup_x_for_positions(nc.scalar.copy, 1, range(quarter, quarter + 1))
        for b in range(AHEAD):
            cosines(b)
        turn_v(AHEAD)

        weigh(0, 0)
        weigh(0, 1)
        quantise_weighted(0, 0)
        cosines(2)
        turn_v(3)
        weigh(1, 0)
        quantise_weighted(0, 1)
        weigh(1, 1)
        quantise_weighted(1, 0)
        quantise_x_along_positions(1)
        cosines(3, passes=(1, 0))
        bring_to_sbuf(3, 1)
        weigh(3, 1)
        turn_v(4)
        turn_v(5)
        cosines(5, passes=(1,))
        bring_to_sbuf(5, 1)
        project(0)

        for b in (2, 4):
            weigh(b, 0)
            weigh(b, 1)
            weigh(b + 1, 0)
            quantise_weighted(b - 1, 1)
            quantise_weighted(b, 0)
            quantise_weighted(b, 1)
            quantise_weighted(b + 1, 0)
            cosines(b + 2)
            if b == 2:
                weigh(b + 3, 1)
                cosines(b + 3, passes=(0,))
                turn_v(6)
                turn_v(7)
            else:
                project(b - 2)
                cosines(b + 3)
            project(b - 1)
            if b == 4:
                project(b)

        weigh(6, 0)
        quantise_weighted(5, 1)
        weigh(6, 1)
        quantise_weighted(6, 0)
        project(5)
        weigh(7, 0)
        quantise_weighted(6, 1)
        weigh(7, 1)
        quantise_weighted(7, 0)
        quantise_weighted(7, 1)
        project(6, copy=nc.vector.tensor_copy)
        project_in_halves(7)
